import numpy as np
import ml_dtypes


def mxq(x, axis, fmt="e4m3"):
    dtype, down = {"e4m3": (ml_dtypes.float8_e4m3fn, 7), "e5m2": (ml_dtypes.float8_e5m2, 14)}[fmt]
    v = np.moveaxis(np.asarray(x, np.float32).astype(ml_dtypes.bfloat16).astype(np.float64), axis, -1)
    blocks = v.reshape(v.shape[:-1] + (-1, 32))
    amax = np.abs(blocks).max(-1, keepdims=True)
    byte = np.maximum(np.where(amax > 0, np.frexp(amax)[1] - 1 + 127, 0) - down, 1)
    scale = np.exp2(byte - 127.0)
    codes = (blocks / scale).astype(np.float32).astype(dtype).astype(np.float64)
    return np.moveaxis((codes * scale).reshape(v.shape), -1, axis)


WIDE = False


def mx_kscale(k):
    if not WIDE:
        return np.ones(k)
    levels = np.array([20, -20, 10, -10, 0])
    a = np.random.permutation(np.resize(levels, k // 512 * 4)).reshape(k // 512, 4)
    idx = np.arange(k)
    return np.exp2(a[idx // 512, idx % 128 // 32])


BF16 = ml_dtypes.bfloat16


def bf(x):
    return np.asarray(x, np.float32).astype(BF16)


def f64(x):
    return np.asarray(x).astype(np.float64)


B, C, ROWS, COLS, H, W = 64, 16, 64, 64, 32, 32
T = B * C
K = ROWS * COLS
N = H * W
DENSITY = 0.1


def setup_inputs():
    s = mx_kscale(T)[:, None]
    image = np.random.standard_normal((T, K)) * s
    votes = (np.random.random_sample((K, N)) < DENSITY) * (1.0 + 0.25 * np.random.standard_normal((K, N)))
    g = np.random.standard_normal((T, N)) * np.exp2(np.random.randint(-12, 1, (T, 1))) * 16.0 / s
    return {"image": bf(image.reshape(B, C, ROWS, COLS)),
            "vote_index": bf(votes.reshape(ROWS, COLS, H, W)),
            "grad_out": bf(g.reshape(B, C, H, W))}


def reference(image, vote_index, grad_out):
    rows, cols, h, w = vote_index.shape
    b, c = image.shape[0], image.shape[1]
    x = np.maximum(f64(image).reshape(b * c, rows * cols), 0.0)
    g = f64(grad_out).reshape(b * c, h * w)
    dV = (mxq(x, 0, "e4m3").T @ mxq(g, 0, "e5m2")) / cols
    return dV.reshape(rows, cols, h, w)

@@ -1,0 +1,112 @@
+import concourse.mybir as mybir
+
+F32 = mybir.dt.float32
+BF16 = mybir.dt.bfloat16
+U32 = mybir.dt.uint32
+U8 = mybir.dt.uint8
+E4M3X4 = mybir.dt.float8_e4m3fn_x4
+E5M2X4 = mybir.dt.float8_e5m2_x4
+
+P = 128
+PACK = 4
+T = 1024
+PASSES = T // (P * PACK)
+KX = 4096
+N = 1024
+N_TILE = 512
+GROUP = 512
+TILES = GROUP // P
+LOAD_COLS = 1024
+STAGE_BUFS = 5
+
+FLOPS = 2 * T * KX * N
+BYTES = T * KX * 2 + T * N * 2 + KX * N * 4
+
+
+def regroup(dst, src):
+    return (
+        dst.rearrange("p (c i) t -> p c t i", i=4),
+        src.rearrange("p t (c i) -> p c t i", i=4),
+    )
+
+
+def tile_ht_kernel(tc, image, vote_index, grad_out, out):
+    nc = tc.nc
+    x_dram = image.rearrange("b c r w -> (b c) (r w)").rearrange("(s p j) k -> p s j k", s=PASSES, j=PACK)
+    g_dram = grad_out.rearrange("b c h w -> (b c) (h w)").rearrange("(s p j) n -> p s j n", s=PASSES, j=PACK)
+    out_dram = out.rearrange("r c h w -> (r c) (h w)").rearrange("(q i m) n -> q m i n", i=TILES, m=P)
+    groups = KX // GROUP
+    blocks = KX // LOAD_COLS
+
+    with tc.tile_pool(name="raw", bufs=1) as raw_pool, tc.tile_pool(name="keep", bufs=1) as keep, tc.tile_pool(
+        name="grp", bufs=4
+    ) as grp_pool, tc.tile_pool(name="cod", bufs=3) as cod_pool, tc.tile_pool(
+        name="stg", bufs=STAGE_BUFS
+    ) as stg_pool, tc.psum_pool(name="acc", bufs=8) as psum:
+        g_raw = []
+        for s in range(PASSES):
+            t = raw_pool.tile([P, PACK, N], BF16, name="g_raw%d" % s)
+            nc.sync.dma_start(out=t[:], in_=g_dram[:, s])
+            g_raw.append(t)
+        x_raw = []
+        for b in range(blocks):
+            pair = []
+            for s in range(PASSES):
+                t = raw_pool.tile([P, PACK, LOAD_COLS], BF16, name="x_raw%d_%d" % (b, s))
+                nc.sync.dma_start(out=t[:], in_=x_dram[:, s, :, b * LOAD_COLS : (b + 1) * LOAD_COLS])
+                pair.append(t)
+            x_raw.append(pair)
+
+        g_codes = keep.tile([P, PASSES, N], U32, name="g_codes", align_bytes=64)
+        g_scales = keep.tile([P, PASSES, N], U8, name="g_scales", align_bytes=64)
+        g_grouped = []
+        for s in range(PASSES):
+            grouped = grp_pool.tile([P, N, PACK], BF16, name="grouped", align_bytes=64)
+            dst, src = regroup(grouped[:], g_raw[s][:])
+            nc.vector.tensor_copy(out=dst, in_=src)
+            g_grouped.append(grouped)
+        for s in range(PASSES):
+            nc.vector.quantize_mx(
+                out=g_codes[:, s, :].bitcast(E5M2X4),
+                scales=g_scales[:, s, :],
+                in_=g_grouped[s][:].rearrange("p w j -> p (w j)"),
+            )
+
+        def regroup_x(q):
+            grouped = grp_pool.tile([P, PASSES * GROUP, PACK], BF16, name="grouped", align_bytes=64)
+            b = (q * GROUP) // LOAD_COLS
+            c0 = (q * GROUP) % LOAD_COLS
+            for s in range(PASSES):
+                dst, src = regroup(grouped[:, s * GROUP : (s + 1) * GROUP, :], x_raw[b][s][:, :, c0 : c0 + GROUP])
+                nc.vector.tensor_scalar_max(out=dst, in0=src, scalar1=0.0)
+            return grouped
+
+        nxt = regroup_x(0)
+        for q in range(groups):
+            grouped = nxt
+            if q + 1 < groups:
+                nxt = regroup_x(q + 1)
+            codes = cod_pool.tile([P, PASSES * GROUP], U32, name="codes", align_bytes=64)
+            scales = cod_pool.tile([P, PASSES * GROUP], U8, name="scales", align_bytes=64)
+            nc.vector.quantize_mx(
+                out=codes[:].bitcast(E4M3X4),
+                scales=scales[:],
+                in_=grouped[:].rearrange("p w j -> p (w j)"),
+            )
+            stage = stg_pool.tile([P, TILES, N], F32, name="stage")
+            for i in range(TILES):
+                for h in range(N // N_TILE):
+                    acc = psum.tile([P, N_TILE], F32, name="acc")
+                    for s in range(PASSES):
+                        m0 = s * GROUP + i * P
+                        nc.tensor.matmul_mx(
+                            out=acc[:],
+                            lhsT=codes[:, m0 : m0 + P].bitcast(E4M3X4),
+                            lhsT_scale=scales[:, m0 : m0 + P],
+                            rhs=g_codes[:, s, h * N_TILE : (h + 1) * N_TILE].bitcast(E5M2X4),
+                            rhs_scale=g_scales[:, s, h * N_TILE : (h + 1) * N_TILE],
+                            start=(s == 0),
+                            stop=(s == PASSES - 1),
+                        )
+                    nc.scalar.mul(out=stage[:, i, h * N_TILE : (h + 1) * N_TILE], in_=acc[:], mul=1.0 / 64.0)
+            nc.sync.dma_start(out=out_dram[q], in_=stage[:])

@@ -14,29 +14,24 @@ PASSES = T // (P * PACK)
 KX = 4096
 N = 1024
 N_TILE = 512
+HALVES = N // N_TILE
 GROUP = 512
 TILES = GROUP // P
-LOAD_COLS = 1024
+BLOCKS = (1024, 1024, 2048)
 STAGE_BUFS = 5
+G_VECTOR_COLS = 672
+VECTOR_BANK = (1, 0)
 
 FLOPS = 2 * T * KX * N
 BYTES = T * KX * 2 + T * N * 2 + KX * N * 4
-
-
-def regroup(dst, src):
-    return (
-        dst.rearrange("p (c i) t -> p c t i", i=4),
-        src.rearrange("p t (c i) -> p c t i", i=4),
-    )
 
 
 def tile_ht_kernel(tc, image, vote_index, grad_out, out):
     nc = tc.nc
     x_dram = image.rearrange("b c r w -> (b c) (r w)").rearrange("(s p j) k -> p s j k", s=PASSES, j=PACK)
     g_dram = grad_out.rearrange("b c h w -> (b c) (h w)").rearrange("(s p j) n -> p s j n", s=PASSES, j=PACK)
-    out_dram = out.rearrange("r c h w -> (r c) (h w)").rearrange("(q i m) n -> q m i n", i=TILES, m=P)
+    out_dram = out.rearrange("r c h w -> (r c) (h w)").rearrange("(q m i) n -> q m i n", m=P, i=TILES)
     groups = KX // GROUP
-    blocks = KX // LOAD_COLS
 
     with tc.tile_pool(name="raw", bufs=1) as raw_pool, tc.tile_pool(name="keep", bufs=1) as keep, tc.tile_pool(
         name="grp", bufs=4
@@ -48,65 +43,88 @@ def tile_ht_kernel(tc, image, vote_index, grad_out, out):
             t = raw_pool.tile([P, PACK, N], BF16, name="g_raw%d" % s)
             nc.sync.dma_start(out=t[:], in_=g_dram[:, s])
             g_raw.append(t)
-        x_raw = []
-        for b in range(blocks):
+        x_src = {}
+        col = 0
+        for b, width in enumerate(BLOCKS):
             pair = []
             for s in range(PASSES):
-                t = raw_pool.tile([P, PACK, LOAD_COLS], BF16, name="x_raw%d_%d" % (b, s))
-                nc.sync.dma_start(out=t[:], in_=x_dram[:, s, :, b * LOAD_COLS : (b + 1) * LOAD_COLS])
+                t = raw_pool.tile([P, PACK, width], BF16, name="x_raw%d_%d" % (b, s))
+                nc.sync.dma_start(out=t[:], in_=x_dram[:, s, :, col : col + width])
                 pair.append(t)
-            x_raw.append(pair)
+            for c0 in range(0, width, GROUP):
+                x_src[(col + c0) // GROUP] = (pair, c0)
+            col += width
 
         g_codes = keep.tile([P, PASSES, N], U32, name="g_codes", align_bytes=64)
         g_scales = keep.tile([P, PASSES, N], U8, name="g_scales", align_bytes=64)
-        g_grouped = []
         for s in range(PASSES):
             grouped = grp_pool.tile([P, N, PACK], BF16, name="grouped", align_bytes=64)
-            dst, src = regroup(grouped[:], g_raw[s][:])
-            nc.vector.tensor_copy(out=dst, in_=src)
-            g_grouped.append(grouped)
-        for s in range(PASSES):
+            a = G_VECTOR_COLS
+            nc.vector.tensor_copy(
+                out=grouped[:, 0:a, :].rearrange("p (c i) t -> p c t i", i=4),
+                in_=g_raw[s][:, :, 0:a].rearrange("p t (c i) -> p c t i", i=4),
+            )
+            nc.scalar.copy(
+                out=grouped[:, a:N, :].rearrange("p (c i) t -> p c t i", i=4),
+                in_=g_raw[s][:, :, a:N].rearrange("p t (c i) -> p c t i", i=4),
+            )
             nc.vector.quantize_mx(
                 out=g_codes[:, s, :].bitcast(E5M2X4),
                 scales=g_scales[:, s, :],
-                in_=g_grouped[s][:].rearrange("p w j -> p (w j)"),
+                in_=grouped[:].rearrange("p w j -> p (w j)"),
             )
 
         def regroup_x(q):
-            grouped = grp_pool.tile([P, PASSES * GROUP, PACK], BF16, name="grouped", align_bytes=64)
-            b = (q * GROUP) // LOAD_COLS
-            c0 = (q * GROUP) % LOAD_COLS
+            grouped = grp_pool.tile([P, TILES, PASSES, P, PACK], BF16, name="grouped", align_bytes=64)
+            pair, c0 = x_src[q]
             for s in range(PASSES):
-                dst, src = regroup(grouped[:, s * GROUP : (s + 1) * GROUP, :], x_raw[b][s][:, :, c0 : c0 + GROUP])
-                nc.vector.tensor_scalar_max(out=dst, in0=src, scalar1=0.0)
+                nc.vector.tensor_scalar_max(
+                    out=grouped[:, :, s, :, :].rearrange("p i m j -> p m j i"),
+                    in0=pair[s][:, :, c0 : c0 + GROUP].rearrange("p j (m i) -> p m j i", i=TILES),
+                    scalar1=0.0,
+                )
             return grouped
 
-        nxt = regroup_x(0)
-        for q in range(groups):
-            grouped = nxt
-            if q + 1 < groups:
-                nxt = regroup_x(q + 1)
-            codes = cod_pool.tile([P, PASSES * GROUP], U32, name="codes", align_bytes=64)
-            scales = cod_pool.tile([P, PASSES * GROUP], U8, name="scales", align_bytes=64)
-            nc.vector.quantize_mx(
-                out=codes[:].bitcast(E4M3X4),
-                scales=scales[:],
-                in_=grouped[:].rearrange("p w j -> p (w j)"),
-            )
+        def quantise_x(grouped, pieces):
+            codes = cod_pool.tile([P, TILES, PASSES, P], U32, name="codes", align_bytes=64)
+            scales = cod_pool.tile([P, TILES, PASSES, P], U8, name="scales", align_bytes=64)
+            step = TILES // pieces
+            for i0 in range(0, TILES, step):
+                nc.vector.quantize_mx(
+                    out=codes[:, i0 : i0 + step].rearrange("p i s m -> p (i s m)").bitcast(E4M3X4),
+                    scales=scales[:, i0 : i0 + step].rearrange("p i s m -> p (i s m)"),
+                    in_=grouped[:, i0 : i0 + step].rearrange("p i s m j -> p (i s m j)"),
+                )
+            return codes, scales
+
+        def multiply(q, codes, scales):
             stage = stg_pool.tile([P, TILES, N], F32, name="stage")
             for i in range(TILES):
-                for h in range(N // N_TILE):
+                for h in range(HALVES):
                     acc = psum.tile([P, N_TILE], F32, name="acc")
                     for s in range(PASSES):
-                        m0 = s * GROUP + i * P
                         nc.tensor.matmul_mx(
                             out=acc[:],
-                            lhsT=codes[:, m0 : m0 + P].bitcast(E4M3X4),
-                            lhsT_scale=scales[:, m0 : m0 + P],
+                            lhsT=codes[:, i, s, :].bitcast(E4M3X4),
+                            lhsT_scale=scales[:, i, s, :],
                             rhs=g_codes[:, s, h * N_TILE : (h + 1) * N_TILE].bitcast(E5M2X4),
                             rhs_scale=g_scales[:, s, h * N_TILE : (h + 1) * N_TILE],
                             start=(s == 0),
                             stop=(s == PASSES - 1),
                         )
-                    nc.scalar.mul(out=stage[:, i, h * N_TILE : (h + 1) * N_TILE], in_=acc[:], mul=1.0 / 64.0)
+                    dst = stage[:, i, h * N_TILE : (h + 1) * N_TILE]
+                    if (i, h) == VECTOR_BANK:
+                        nc.vector.tensor_scalar_mul(out=dst, in0=acc[:], scalar1=1.0 / 64.0)
+                    else:
+                        nc.scalar.mul(out=dst, in_=acc[:], mul=1.0 / 64.0)
             nc.sync.dma_start(out=out_dram[q], in_=stage[:])
+
+        grouped = regroup_x(0)
+        ready = quantise_x(grouped, 2)
+        grouped = regroup_x(1)
+        for q in range(groups):
+            nxt = regroup_x(q + 2) if q + 2 < groups else None
+            multiply(q, ready[0], ready[1])
+            if q + 1 < groups:
+                ready = quantise_x(grouped, 1)
+            grouped = nxt

@@ -37,7 +37,7 @@ def tile_ht_kernel(tc, image, vote_index, grad_out, out):
         name="grp", bufs=4
     ) as grp_pool, tc.tile_pool(name="cod", bufs=3) as cod_pool, tc.tile_pool(
         name="stg", bufs=STAGE_BUFS
-    ) as stg_pool, tc.psum_pool(name="acc", bufs=8) as psum:
+    ) as stg_pool, tc.psum_pool(name="acc", bufs=8) as psum, tc.manual_schedule():
         g_raw = []
         for s in range(PASSES):
             t = raw_pool.tile([P, PACK, N], BF16, name="g_raw%d" % s)
@@ -99,6 +99,7 @@ def tile_ht_kernel(tc, image, vote_index, grad_out, out):
 
         def multiply(q, codes, scales):
             stage = stg_pool.tile([P, TILES, N], F32, name="stage")
+            left = None
             for i in range(TILES):
                 for h in range(HALVES):
                     acc = psum.tile([P, N_TILE], F32, name="acc")
@@ -114,17 +115,20 @@ def tile_ht_kernel(tc, image, vote_index, grad_out, out):
                         )
                     dst = stage[:, i, h * N_TILE : (h + 1) * N_TILE]
                     if (i, h) == VECTOR_BANK:
-                        nc.vector.tensor_scalar_mul(out=dst, in0=acc[:], scalar1=1.0 / 64.0)
+                        left = (dst, acc)
                     else:
                         nc.scalar.mul(out=dst, in_=acc[:], mul=1.0 / 64.0)
-            nc.sync.dma_start(out=out_dram[q], in_=stage[:])
+            return stage, left
 
-        grouped = regroup_x(0)
-        ready = quantise_x(grouped, 2)
-        grouped = regroup_x(1)
+        def finish(q, stage, left, pieces):
+            nc.vector.tensor_scalar_mul(out=left[0], in0=left[1][:], scalar1=1.0 / 64.0)
+            step = TILES // pieces
+            for i0 in range(0, TILES, step):
+                nc.sync.dma_start(out=out_dram[q][:, i0 : i0 + step, :], in_=stage[:, i0 : i0 + step, :])
+
+        ready = quantise_x(regroup_x(0), 2)
         for q in range(groups):
-            nxt = regroup_x(q + 2) if q + 2 < groups else None
-            multiply(q, ready[0], ready[1])
+            stage, left = multiply(q, ready[0], ready[1])
             if q + 1 < groups:
-                ready = quantise_x(grouped, 1)
-            grouped = nxt
+                ready = quantise_x(regroup_x(q + 1), 1)
+            finish(q, stage, left, 2 if q == groups - 1 else 1)

@@ -17,10 +17,10 @@ N_TILE = 512
 HALVES = N // N_TILE
 GROUP = 512
 TILES = GROUP // P
-BLOCKS = (1024, 1024, 2048)
+BLOCKS = (1536, 2560)
 STAGE_BUFS = 5
 G_VECTOR_COLS = 672
-VECTOR_BANK = (1, 0)
+VECTOR_BANK = None
 
 FLOPS = 2 * T * KX * N
 BYTES = T * KX * 2 + T * N * 2 + KX * N * 4
@@ -121,7 +121,8 @@ def tile_ht_kernel(tc, image, vote_index, grad_out, out):
             return stage, left
 
         def finish(q, stage, left, pieces):
-            nc.vector.tensor_scalar_mul(out=left[0], in0=left[1][:], scalar1=1.0 / 64.0)
+            if left is not None:
+                nc.vector.tensor_scalar_mul(out=left[0], in0=left[1][:], scalar1=1.0 / 64.0)
             step = TILES // pieces
             for i0 in range(0, TILES, step):
                 nc.sync.dma_start(out=out_dram[q][:, i0 : i0 + step, :], in_=stage[:, i0 : i0 + step, :])

@@ -6,6 +6,7 @@ U32 = mybir.dt.uint32
 U8 = mybir.dt.uint8
 E4M3X4 = mybir.dt.float8_e4m3fn_x4
 E5M2X4 = mybir.dt.float8_e5m2_x4
+RELU = mybir.ActivationFunctionType.Relu
 
 P = 128
 PACK = 4
@@ -20,7 +21,6 @@ TILES = GROUP // P
 BLOCKS = (1536, 2560)
 STAGE_BUFS = 5
 G_VECTOR_COLS = 672
-VECTOR_BANK = None
 
 FLOPS = 2 * T * KX * N
 BYTES = T * KX * 2 + T * N * 2 + KX * N * 4
@@ -38,26 +38,32 @@ def tile_ht_kernel(tc, image, vote_index, grad_out, out):
     ) as grp_pool, tc.tile_pool(name="cod", bufs=3) as cod_pool, tc.tile_pool(
         name="stg", bufs=STAGE_BUFS
     ) as stg_pool, tc.psum_pool(name="acc", bufs=8) as psum, tc.manual_schedule():
-        g_raw = []
-        for s in range(PASSES):
+        g_raw = {}
+        x_raw = {}
+        starts = [sum(BLOCKS[:b]) for b in range(len(BLOCKS))]
+
+        def load_g(s):
             t = raw_pool.tile([P, PACK, N], BF16, name="g_raw%d" % s)
             nc.sync.dma_start(out=t[:], in_=g_dram[:, s])
-            g_raw.append(t)
-        x_src = {}
-        col = 0
-        for b, width in enumerate(BLOCKS):
-            pair = []
+            g_raw[s] = t
+
+        def load_x(b, s):
+            t = raw_pool.tile([P, PACK, BLOCKS[b]], BF16, name="x_raw%d_%d" % (b, s))
+            nc.sync.dma_start(out=t[:], in_=x_dram[:, s, :, starts[b] : starts[b] + BLOCKS[b]])
+            x_raw[(b, s)] = t
+
+        load_g(0)
+        load_x(0, 0)
+        load_g(1)
+        load_x(0, 1)
+        for b in range(1, len(BLOCKS)):
             for s in range(PASSES):
-                t = raw_pool.tile([P, PACK, width], BF16, name="x_raw%d_%d" % (b, s))
-                nc.sync.dma_start(out=t[:], in_=x_dram[:, s, :, col : col + width])
-                pair.append(t)
-            for c0 in range(0, width, GROUP):
-                x_src[(col + c0) // GROUP] = (pair, c0)
-            col += width
+                load_x(b, s)
 
         g_codes = keep.tile([P, PASSES, N], U32, name="g_codes", align_bytes=64)
         g_scales = keep.tile([P, PASSES, N], U8, name="g_scales", align_bytes=64)
-        for s in range(PASSES):
+
+        def prepare_g(s):
             grouped = grp_pool.tile([P, N, PACK], BF16, name="grouped", align_bytes=64)
             a = G_VECTOR_COLS
             nc.vector.tensor_copy(
@@ -74,62 +80,80 @@ def tile_ht_kernel(tc, image, vote_index, grad_out, out):
                 in_=grouped[:].rearrange("p w j -> p (w j)"),
             )
 
-        def regroup_x(q):
-            grouped = grp_pool.tile([P, TILES, PASSES, P, PACK], BF16, name="grouped", align_bytes=64)
-            pair, c0 = x_src[q]
-            for s in range(PASSES):
-                nc.vector.tensor_scalar_max(
-                    out=grouped[:, :, s, :, :].rearrange("p i m j -> p m j i"),
-                    in0=pair[s][:, :, c0 : c0 + GROUP].rearrange("p j (m i) -> p m j i", i=TILES),
-                    scalar1=0.0,
-                )
-            return grouped
+        def new_group():
+            grouped = grp_pool.tile([P, PASSES, TILES, P, PACK], BF16, name="grouped", align_bytes=64)
+            codes = cod_pool.tile([P, PASSES, TILES, P], U32, name="codes", align_bytes=64)
+            scales = cod_pool.tile([P, PASSES, TILES, P], U8, name="scales", align_bytes=64)
+            return grouped, codes, scales
 
-        def quantise_x(grouped, pieces):
-            codes = cod_pool.tile([P, TILES, PASSES, P], U32, name="codes", align_bytes=64)
-            scales = cod_pool.tile([P, TILES, PASSES, P], U8, name="scales", align_bytes=64)
-            step = TILES // pieces
-            for i0 in range(0, TILES, step):
-                nc.vector.quantize_mx(
-                    out=codes[:, i0 : i0 + step].rearrange("p i s m -> p (i s m)").bitcast(E4M3X4),
-                    scales=scales[:, i0 : i0 + step].rearrange("p i s m -> p (i s m)"),
-                    in_=grouped[:, i0 : i0 + step].rearrange("p i s m j -> p (i s m j)"),
-                )
-            return codes, scales
+        def regroup_x(unit, q, s, on_scalar=False):
+            b = max(k for k in range(len(BLOCKS)) if starts[k] <= q * GROUP)
+            c0 = q * GROUP - starts[b]
+            dst = unit[0][:, s].rearrange("p i m j -> p m j i")
+            src = x_raw[(b, s)][:, :, c0 : c0 + GROUP].rearrange("p j (m i) -> p m j i", i=TILES)
+            if on_scalar:
+                nc.scalar.activation(out=dst, in_=src, func=RELU)
+            else:
+                nc.vector.tensor_scalar_max(out=dst, in0=src, scalar1=0.0)
 
-        def multiply(q, codes, scales):
-            stage = stg_pool.tile([P, TILES, N], F32, name="stage")
-            left = None
-            for i in range(TILES):
-                for h in range(HALVES):
-                    acc = psum.tile([P, N_TILE], F32, name="acc")
-                    for s in range(PASSES):
-                        nc.tensor.matmul_mx(
-                            out=acc[:],
-                            lhsT=codes[:, i, s, :].bitcast(E4M3X4),
-                            lhsT_scale=scales[:, i, s, :],
-                            rhs=g_codes[:, s, h * N_TILE : (h + 1) * N_TILE].bitcast(E5M2X4),
-                            rhs_scale=g_scales[:, s, h * N_TILE : (h + 1) * N_TILE],
-                            start=(s == 0),
-                            stop=(s == PASSES - 1),
-                        )
-                    dst = stage[:, i, h * N_TILE : (h + 1) * N_TILE]
-                    if (i, h) == VECTOR_BANK:
-                        left = (dst, acc)
-                    else:
-                        nc.scalar.mul(out=dst, in_=acc[:], mul=1.0 / 64.0)
-            return stage, left
+        def quantise_x(unit, s0, s1):
+            grouped, codes, scales = unit
+            nc.vector.quantize_mx(
+                out=codes[:, s0:s1].rearrange("p s i m -> p (s i m)").bitcast(E4M3X4),
+                scales=scales[:, s0:s1].rearrange("p s i m -> p (s i m)"),
+                in_=grouped[:, s0:s1].rearrange("p s i m j -> p (s i m j)"),
+            )
 
-        def finish(q, stage, left, pieces):
-            if left is not None:
-                nc.vector.tensor_scalar_mul(out=left[0], in0=left[1][:], scalar1=1.0 / 64.0)
+        def one_pass(unit, acc, i, h, s):
+            nc.tensor.matmul_mx(
+                out=acc[:],
+                lhsT=unit[1][:, s, i, :].bitcast(E4M3X4),
+                lhsT_scale=unit[2][:, s, i, :],
+                rhs=g_codes[:, s, h * N_TILE : (h + 1) * N_TILE].bitcast(E5M2X4),
+                rhs_scale=g_scales[:, s, h * N_TILE : (h + 1) * N_TILE],
+                start=(s == 0),
+                stop=(s == PASSES - 1),
+            )
+
+        def empty(stage, acc, i, h):
+            nc.scalar.mul(out=stage[:, i, h * N_TILE : (h + 1) * N_TILE], in_=acc[:], mul=1.0 / 64.0)
+
+        def store(q, stage, pieces):
             step = TILES // pieces
             for i0 in range(0, TILES, step):
                 nc.sync.dma_start(out=out_dram[q][:, i0 : i0 + step, :], in_=stage[:, i0 : i0 + step, :])
 
-        ready = quantise_x(regroup_x(0), 2)
-        for q in range(groups):
-            stage, left = multiply(q, ready[0], ready[1])
+        banks = [(i, h) for i in range(TILES) for h in range(HALVES)]
+
+        unit0 = new_group()
+        unit1 = new_group()
+        accs = {}
+        stage = stg_pool.tile([P, TILES, N], F32, name="stage")
+        for s in range(PASSES):
+            prepare_g(s)
+            regroup_x(unit0, 0, s)
+            regroup_x(unit1, 1, s, on_scalar=True)
+            quantise_x(unit0, s, s + 1)
+            for i, h in banks:
+                if s == 0:
+                    accs[(i, h)] = psum.tile([P, N_TILE], F32, name="acc")
+                one_pass(unit0, accs[(i, h)], i, h, s)
+                if s == PASSES - 1:
+                    empty(stage, accs[(i, h)], i, h)
+        quantise_x(unit1, 0, PASSES)
+        store(0, stage, 1)
+
+        ready = unit1
+        for q in range(1, groups):
+            stage = stg_pool.tile([P, TILES, N], F32, name="stage")
+            for i, h in banks:
+                acc = psum.tile([P, N_TILE], F32, name="acc")
+                for s in range(PASSES):
+                    one_pass(ready, acc, i, h, s)
+                empty(stage, acc, i, h)
             if q + 1 < groups:
-                ready = quantise_x(regroup_x(q + 1), 1)
-            finish(q, stage, left, 2 if q == groups - 1 else 1)
+                ready = new_group()
+                for s in range(PASSES):
+                    regroup_x(ready, q + 1, s)
+                quantise_x(ready, 0, PASSES)
+            store(q, stage, 2 if q == groups - 1 else 1)

import concourse.mybir as mybir

F32 = mybir.dt.float32
BF16 = mybir.dt.bfloat16
U32 = mybir.dt.uint32
U8 = mybir.dt.uint8
E4M3X4 = mybir.dt.float8_e4m3fn_x4
E5M2X4 = mybir.dt.float8_e5m2_x4
RELU = mybir.ActivationFunctionType.Relu

P = 128
PACK = 4
T = 1024
PASSES = T // (P * PACK)
KX = 4096
N = 1024
N_TILE = 512
HALVES = N // N_TILE
GROUP = 512
TILES = GROUP // P
BLOCKS = (1536, 2560)
STAGE_BUFS = 5
G_VECTOR_COLS = 672

FLOPS = 2 * T * KX * N
BYTES = T * KX * 2 + T * N * 2 + KX * N * 4


def tile_ht_kernel(tc, image, vote_index, grad_out, out):
    nc = tc.nc
    x_dram = image.rearrange("b c r w -> (b c) (r w)").rearrange("(s p j) k -> p s j k", s=PASSES, j=PACK)
    g_dram = grad_out.rearrange("b c h w -> (b c) (h w)").rearrange("(s p j) n -> p s j n", s=PASSES, j=PACK)
    out_dram = out.rearrange("r c h w -> (r c) (h w)").rearrange("(q m i) n -> q m i n", m=P, i=TILES)
    groups = KX // GROUP

    with tc.tile_pool(name="raw", bufs=1) as raw_pool, tc.tile_pool(name="keep", bufs=1) as keep, tc.tile_pool(
        name="grp", bufs=4
    ) as grp_pool, tc.tile_pool(name="cod", bufs=3) as cod_pool, tc.tile_pool(
        name="stg", bufs=STAGE_BUFS
    ) as stg_pool, tc.psum_pool(name="acc", bufs=8) as psum, tc.manual_schedule():
        g_raw = {}
        x_raw = {}
        starts = [sum(BLOCKS[:b]) for b in range(len(BLOCKS))]

        def load_g(s):
            t = raw_pool.tile([P, PACK, N], BF16, name="g_raw%d" % s)
            nc.sync.dma_start(out=t[:], in_=g_dram[:, s])
            g_raw[s] = t

        def load_x(b, s):
            t = raw_pool.tile([P, PACK, BLOCKS[b]], BF16, name="x_raw%d_%d" % (b, s))
            nc.sync.dma_start(out=t[:], in_=x_dram[:, s, :, starts[b] : starts[b] + BLOCKS[b]])
            x_raw[(b, s)] = t

        load_g(0)
        load_x(0, 0)
        load_g(1)
        load_x(0, 1)
        for b in range(1, len(BLOCKS)):
            for s in range(PASSES):
                load_x(b, s)

        g_codes = keep.tile([P, PASSES, N], U32, name="g_codes", align_bytes=64)
        g_scales = keep.tile([P, PASSES, N], U8, name="g_scales", align_bytes=64)

        def prepare_g(s):
            grouped = grp_pool.tile([P, N, PACK], BF16, name="grouped", align_bytes=64)
            a = G_VECTOR_COLS
            nc.vector.tensor_copy(
                out=grouped[:, 0:a, :].rearrange("p (c i) t -> p c t i", i=4),
                in_=g_raw[s][:, :, 0:a].rearrange("p t (c i) -> p c t i", i=4),
            )
            nc.scalar.copy(
                out=grouped[:, a:N, :].rearrange("p (c i) t -> p c t i", i=4),
                in_=g_raw[s][:, :, a:N].rearrange("p t (c i) -> p c t i", i=4),
            )
            nc.vector.quantize_mx(
                out=g_codes[:, s, :].bitcast(E5M2X4),
                scales=g_scales[:, s, :],
                in_=grouped[:].rearrange("p w j -> p (w j)"),
            )

        def new_group():
            grouped = grp_pool.tile([P, PASSES, TILES, P, PACK], BF16, name="grouped", align_bytes=64)
            codes = cod_pool.tile([P, PASSES, TILES, P], U32, name="codes", align_bytes=64)
            scales = cod_pool.tile([P, PASSES, TILES, P], U8, name="scales", align_bytes=64)
            return grouped, codes, scales

        def regroup_x(unit, q, s, on_scalar=False):
            b = max(k for k in range(len(BLOCKS)) if starts[k] <= q * GROUP)
            c0 = q * GROUP - starts[b]
            dst = unit[0][:, s].rearrange("p i m j -> p m j i")
            src = x_raw[(b, s)][:, :, c0 : c0 + GROUP].rearrange("p j (m i) -> p m j i", i=TILES)
            if on_scalar:
                nc.scalar.activation(out=dst, in_=src, func=RELU)
            else:
                nc.vector.tensor_scalar_max(out=dst, in0=src, scalar1=0.0)

        def quantise_x(unit, s0, s1):
            grouped, codes, scales = unit
            nc.vector.quantize_mx(
                out=codes[:, s0:s1].rearrange("p s i m -> p (s i m)").bitcast(E4M3X4),
                scales=scales[:, s0:s1].rearrange("p s i m -> p (s i m)"),
                in_=grouped[:, s0:s1].rearrange("p s i m j -> p (s i m j)"),
            )

        def one_pass(unit, acc, i, h, s):
            nc.tensor.matmul_mx(
                out=acc[:],
                lhsT=unit[1][:, s, i, :].bitcast(E4M3X4),
                lhsT_scale=unit[2][:, s, i, :],
                rhs=g_codes[:, s, h * N_TILE : (h + 1) * N_TILE].bitcast(E5M2X4),
                rhs_scale=g_scales[:, s, h * N_TILE : (h + 1) * N_TILE],
                start=(s == 0),
                stop=(s == PASSES - 1),
            )

        def empty(stage, acc, i, h):
            nc.scalar.mul(out=stage[:, i, h * N_TILE : (h + 1) * N_TILE], in_=acc[:], mul=1.0 / 64.0)

        def store(q, stage, pieces):
            step = TILES // pieces
            for i0 in range(0, TILES, step):
                nc.sync.dma_start(out=out_dram[q][:, i0 : i0 + step, :], in_=stage[:, i0 : i0 + step, :])

        banks = [(i, h) for i in range(TILES) for h in range(HALVES)]

        unit0 = new_group()
        unit1 = new_group()
        accs = {}
        stage = stg_pool.tile([P, TILES, N], F32, name="stage")
        for s in range(PASSES):
            prepare_g(s)
            regroup_x(unit0, 0, s)
            regroup_x(unit1, 1, s, on_scalar=True)
            quantise_x(unit0, s, s + 1)
            for i, h in banks:
                if s == 0:
                    accs[(i, h)] = psum.tile([P, N_TILE], F32, name="acc")
                one_pass(unit0, accs[(i, h)], i, h, s)
                if s == PASSES - 1:
                    empty(stage, accs[(i, h)], i, h)
        quantise_x(unit1, 0, PASSES)
        store(0, stage, 1)

        ready = unit1
        for q in range(1, groups):
            stage = stg_pool.tile([P, TILES, N], F32, name="stage")
            for i, h in banks:
                acc = psum.tile([P, N_TILE], F32, name="acc")
                for s in range(PASSES):
                    one_pass(ready, acc, i, h, s)
                empty(stage, acc, i, h)
            if q + 1 < groups:
                ready = new_group()
                for s in range(PASSES):
                    regroup_x(ready, q + 1, s)
                quantise_x(ready, 0, PASSES)
            store(q, stage, 2 if q == groups - 1 else 1)
